import numpy as np
import ml_dtypes


def mxq(x, axis, fmt="e4m3"):
    dtype, down = {"e4m3": (ml_dtypes.float8_e4m3fn, 7), "e5m2": (ml_dtypes.float8_e5m2, 14)}[fmt]
    v = np.moveaxis(np.asarray(x, np.float32).astype(ml_dtypes.bfloat16).astype(np.float64), axis, -1)
    blocks = v.reshape(v.shape[:-1] + (-1, 32))
    amax = np.abs(blocks).max(-1, keepdims=True)
    byte = np.maximum(np.where(amax > 0, np.frexp(amax)[1] - 1 + 127, 0) - down, 1)
    scale = np.exp2(byte - 127.0)
    codes = (blocks / scale).astype(np.float32).astype(dtype).astype(np.float64)
    return np.moveaxis((codes * scale).reshape(v.shape), -1, axis)


WIDE = False


def mx_kscale(k):
    if not WIDE:
        return np.ones(k)
    levels = np.array([10, -10, 5, -5, 0])
    if k % 512:
        return np.exp2(np.random.permutation(np.resize(levels, k // 32))).repeat(32)
    a = np.empty((k // 512, 16))
    for p in range(k // 512):
        a[p, :8] = np.random.permutation(np.resize(levels, 8))
        for g in range(8):
            far = levels[np.abs(levels - a[p, g]) >= 10]
            a[p, g + 8] = far[np.random.randint(len(far))]
    return np.exp2(a.ravel()).repeat(32)


BF16 = ml_dtypes.bfloat16


def bf(x):
    return np.asarray(x, np.float32).astype(BF16)


def f64(x):
    return np.asarray(x).astype(np.float64)


E2M1 = np.array([0.0, 0.5, 1.0, 1.5, 2.0, 3.0, 4.0, 6.0, -0.0, -0.5, -1.0, -1.5, -2.0, -3.0, -4.0, -6.0])


def pack_weight(w, fmt):
    k, n = w.shape
    w = f64(bf(w)).reshape(k // 32, 32, n)
    amax = np.abs(w).max(1)
    if fmt == "e4m3":
        byte = np.frexp(amax)[1] - 1 + 127 - 7
    else:
        mant, ex = np.frexp(amax / 6.0)
        byte = np.where(mant > 0.5, ex, ex - 1) + 127
    byte = np.clip(np.where(amax > 0, byte, 1), 1, 254)
    scaled = (w * np.exp2(127.0 - byte)[:, None, :]).reshape(k, n).astype(np.float32)
    by_word = np.ascontiguousarray(scaled.reshape(k // 512, 128, 4, n).transpose(0, 1, 3, 2))
    if fmt == "e4m3":
        words = by_word.astype(ml_dtypes.float8_e4m3fn).view(np.uint8)
    else:
        c = by_word.astype(ml_dtypes.float4_e2m1fn).view(np.uint8) & 0xF
        words = c[..., 0::2] | (c[..., 1::2] << 4)
    return np.ascontiguousarray(words), np.ascontiguousarray(byte.astype(np.uint8).reshape(k // 512, 16, n))


def unpack_weight(words, scales, fmt):
    g, p, n, _ = words.shape
    if fmt == "e4m3":
        vals = np.ascontiguousarray(words).view(ml_dtypes.float8_e4m3fn).astype(np.float64)
    else:
        nib = np.empty((g, p, n, 4), np.uint8)
        nib[..., 0::2] = words & 0xF
        nib[..., 1::2] = words >> 4
        vals = E2M1[nib]
    vals = vals * np.repeat(np.exp2(scales.astype(np.float64) - 127.0), 8, axis=1)[..., None]
    return vals.transpose(0, 1, 3, 2).reshape(g * 512, n)


B, T, HID, H, NOPE, ROPE, VD, KV_LORA = 1, 512, 2048, 16, 64, 128, 128, 512
HALF = ROPE // 2
EPS = 1e-5


def rope(x, cos, sin):
    c = cos[None, :, None, :]
    s = sin[None, :, None, :]
    x1, x2 = x[..., 0::2], x[..., 1::2]
    o1 = x1 * c - x2 * s
    o2 = x1 * s + x2 * c
    return np.stack([o1, o2], axis=-1).reshape(x.shape)


def layernorm(x, g, b):
    mu = x.mean(-1, keepdims=True)
    var = x.var(-1, keepdims=True)
    return (x - mu) / np.sqrt(var + EPS) * g + b


def draw0():
    s, t = mx_kscale(HID), mx_kscale(KV_LORA)
    ang = np.random.uniform(-np.pi, np.pi, (T, HALF))
    hidden_states = bf(np.random.standard_normal((B, T, HID)) * s)
    Wkv_a_words, Wkv_a_scales = pack_weight(np.random.standard_normal((HID, KV_LORA + ROPE)) / np.sqrt(HID) / s[:, None], "e4m3")
    kv_gamma = bf((1.0 + 0.1 * np.random.standard_normal(KV_LORA)) * t)
    kv_beta = bf(0.1 * np.random.standard_normal(KV_LORA) * t)
    Wkv_b_words, Wkv_b_scales = pack_weight(np.random.standard_normal((KV_LORA, H * (NOPE + VD))) / np.sqrt(KV_LORA) / t[:, None], "e4m3")
    return {"hidden_states": hidden_states,
            "rope_cos": bf(np.cos(ang)), "rope_sin": bf(np.sin(ang)),
            "Wkv_a_words": Wkv_a_words, "Wkv_a_scales": Wkv_a_scales,
            "kv_gamma": kv_gamma,
            "kv_beta": kv_beta,
            "Wkv_b_words": Wkv_b_words, "Wkv_b_scales": Wkv_b_scales}


def core(hidden_states, rope_cos, rope_sin, Wkv_a_words, Wkv_a_scales, kv_gamma, kv_beta, Wkv_b_words, Wkv_b_scales):
    kv = mxq(f64(hidden_states), 2, "e4m3") @ unpack_weight(Wkv_a_words, Wkv_a_scales, "e4m3")
    kv_lat, k_rope = kv[..., :KV_LORA], kv[..., KV_LORA:]
    k_rope = rope(k_rope[:, :, None, :], f64(rope_cos), f64(rope_sin))
    kv_lat = layernorm(kv_lat, f64(kv_gamma), f64(kv_beta))
    kvb = (mxq(kv_lat, 2, "e4m3") @ unpack_weight(Wkv_b_words, Wkv_b_scales, "e4m3")).reshape(B, T, H, NOPE + VD)
    k_nope, v = kvb[..., :NOPE], kvb[..., NOPE:]
    k = np.concatenate([k_nope, np.broadcast_to(k_rope, (B, T, H, ROPE))], axis=-1)
    return k, v


def e4m3fn_bytes(y):
    return np.clip(np.asarray(y, np.float64), -448.0, 448.0).astype(np.float32).astype(ml_dtypes.float8_e4m3fn).view(np.uint8)


def e4m3fn_values(b):
    return np.asarray(b, np.uint8).view(ml_dtypes.float8_e4m3fn).astype(np.float64)


def setup_inputs():
    d = draw0()
    x0 = np.asarray(d['hidden_states']).astype(np.float64)
    s = (np.max(np.abs(x0), axis=(0, 1), keepdims=True) / 448.0).astype(np.float32)
    out = {}
    for k, v in d.items():
        if k == 'hidden_states':
            out['hidden_states_bytes'] = e4m3fn_bytes(x0 / s.astype(np.float64))
            out['hidden_states_scale'] = s
        else:
            out[k] = v
    return out


def reference(hidden_states_bytes, hidden_states_scale, rope_cos, rope_sin, Wkv_a_words, Wkv_a_scales, kv_gamma, kv_beta, Wkv_b_words, Wkv_b_scales):
    return core(e4m3fn_values(hidden_states_bytes) * hidden_states_scale.astype(np.float64), rope_cos, rope_sin, Wkv_a_words, Wkv_a_scales, kv_gamma, kv_beta, Wkv_b_words, Wkv_b_scales)

@@ -1,0 +1,343 @@
+from contextlib import ExitStack
+
+import concourse.mybir as mybir
+from concourse.masks import make_identity
+
+T, HID, LAT, ROPE = 512, 2048, 512, 128
+HEADS, NOPE, VD = 16, 64, 128
+HEAD = NOPE + VD
+EPS = 1e-5
+FLOPS = 2 * T * HID * (LAT + ROPE) + 2 * T * LAT * HEADS * HEAD
+
+F32 = mybir.dt.float32
+BF16 = mybir.dt.bfloat16
+I32 = mybir.dt.int32
+U32 = mybir.dt.uint32
+U8 = mybir.dt.uint8
+FP8 = mybir.dt.float8_e4m3fn
+FP8X4 = mybir.dt.float8_e4m3fn_x4
+ACT = mybir.ActivationFunctionType
+ALU = mybir.AluOpType
+
+P = 128
+PACK = 4
+KP = P * PACK
+NG = HID // KP
+NT = T // P
+
+
+def tile_multilatentattention_pa_w8_kernel(
+    tc, h_bytes, h_scale, cos, sin, wa_words, wa_scales, gamma, beta, wb_words, wb_scales, out_k, out_v
+):
+    nc = tc.nc
+    with ExitStack() as ctx:
+        keep = ctx.enter_context(tc.tile_pool(name="keep", bufs=1))
+        stage = ctx.enter_context(tc.tile_pool(name="stage", bufs=4))
+        small = ctx.enter_context(tc.tile_pool(name="small", bufs=2))
+        outs = ctx.enter_context(tc.tile_pool(name="outs", bufs=4))
+        ps_x = ctx.enter_context(tc.psum_pool(name="ps_x", bufs=3))
+        ps_kv = ctx.enter_context(tc.psum_pool(name="ps_kv", bufs=1))
+        ps_r = ctx.enter_context(tc.psum_pool(name="ps_r", bufs=1))
+        ps_o = ctx.enter_context(tc.psum_pool(name="ps_o", bufs=3))
+        ctx.enter_context(tc.manual_schedule())
+
+        warm = keep.tile([P, 1], F32, name="warm")
+        nc.vector.memset(warm[:], 1.0)
+        nc.scalar.activation(out=warm[:], in_=warm[:], func=ACT.Abs_reciprocal_sqrt)
+        wa_s = keep.tile([P, LAT + ROPE], U8, name="wa_s", align_bytes=64)
+        wb_s = keep.tile([P, HEADS * HEAD], U8, name="wb_s", align_bytes=64)
+        nc.vector.memset(wa_s[:].bitcast(I32), 0)
+        nc.vector.memset(wb_s[:].bitcast(I32), 0)
+        ident32 = keep.tile([P, P], F32, name="ident32")
+        make_identity(nc, ident32[:])
+        ident = keep.tile([P, P], BF16, name="ident")
+        nc.vector.tensor_copy(out=ident[:], in_=ident32[:])
+
+        hb = [keep.tile([P, HID], U8, name="hb%d" % i) for i in range(NT)]
+        wa = [keep.tile([P, LAT + ROPE], U32, name="wa%d" % g, align_bytes=64) for g in range(NG)]
+        wb = keep.tile([P, HEADS * HEAD], U32, name="wb", align_bytes=64)
+        hs = keep.tile([P, NG, PACK], F32, name="hs")
+        cos_t = keep.tile([P, NT, ROPE // 2], BF16, name="cos_t")
+        sin_t = keep.tile([P, NT, ROPE // 2], BF16, name="sin_t")
+        gam = keep.tile([P, LAT], BF16, name="gam")
+        bet = keep.tile([P, LAT], BF16, name="bet")
+
+        def load_h(i):
+            nc.sync.dma_start(out=hb[i][:], in_=h_bytes[0, i * P : (i + 1) * P, :])
+
+        def load_wa(g):
+            nc.sync.dma_start(out=wa[g][:].bitcast(I32), in_=wa_words[g].rearrange("p n t -> p (n t)").bitcast(I32))
+
+        load_h(0)
+        nc.sync.dma_start(out=hs[:], in_=h_scale.rearrange("a b (g p t) -> p (a b g) t", p=P, t=PACK))
+        for q in range(4):
+            nc.sync.dma_start(out=wa_s[32 * q : 32 * q + 16, :].bitcast(I32), in_=wa_scales[:, 4 * q : 4 * q + 4, :].bitcast(I32))
+        load_wa(0)
+        load_wa(1)
+        load_h(1)
+        load_wa(2)
+        load_wa(3)
+        nc.sync.dma_start(out=gam[:], in_=gamma.partition_broadcast(P))
+        nc.sync.dma_start(out=bet[:], in_=beta.partition_broadcast(P))
+        wb_flat = wb_words[0].rearrange("p n t -> p (n t)").bitcast(I32)
+        half = HEADS * HEAD // 2
+
+        def load_wb(j):
+            nc.sync.dma_start(out=wb[:, j * half : (j + 1) * half].bitcast(I32), in_=wb_flat[:, j * half : (j + 1) * half])
+
+        load_wb(0)
+        nc.sync.dma_start(out=cos_t[:], in_=cos.rearrange("(i p) f -> p i f", p=P))
+        nc.sync.dma_start(out=sin_t[:], in_=sin.rearrange("(i p) f -> p i f", p=P))
+        for q in range(4):
+            nc.sync.dma_start(out=wb_s[32 * q : 32 * q + 4, :].bitcast(I32), in_=wb_scales[0, 4 * q : 4 * q + 4, :].bitcast(I32))
+        load_h(2)
+        load_wb(1)
+        load_h(3)
+
+        xw, xt, pr, hq, hqs, kv, rp = {}, {}, {}, {}, {}, {}, {}
+        mv, rs, y1, lat, lt, lg, lq, lqs = {}, {}, {}, {}, {}, {}, {}, {}
+
+        def widen(i, g, n=1, eng=None):
+            if i >= NT:
+                return
+            x = stage.tile([P, n * KP], BF16, name="xw%d" % n, bufs=8 if n == 1 else 4)
+            for j in range(n):
+                xw[i, g + j] = x[:, j * KP : (j + 1) * KP]
+            src = hb[i][:, g * KP : (g + n) * KP].bitcast(FP8)
+            if eng is None:
+                nc.scalar.copy(out=x[:], in_=src)
+            else:
+                eng.tensor_copy(out=x[:], in_=src)
+
+        def turn(i, g, n=1):
+            if i >= NT:
+                return
+            t = ps_x.tile([P, n, PACK, P], BF16, name="xt", tag="xt")
+            xt[i, g] = t
+            for c in range(n):
+                for j in range(PACK):
+                    nc.tensor.transpose(t[:, c, j, :], xw[i, g + c][:, j : KP : PACK], ident[:])
+
+        def scale(i, g, n=1):
+            if i >= NT:
+                return
+            p = stage.tile([P, n, P, PACK], BF16, name="pr%d" % n, align_bytes=64)
+            pr[i, g] = p
+            nc.vector.tensor_tensor(
+                out=p[:],
+                in0=xt[i, g][:].rearrange("p c t n -> p c n t"),
+                in1=hs[:, g : g + n, :].unsqueeze(2).to_broadcast([P, n, P, PACK]),
+                op=ALU.mult,
+            )
+
+        def quant(i, g, n=1):
+            if i >= NT:
+                return
+            if g == 0:
+                hq[i] = small.tile([P, NG, P], U32, name="hq", align_bytes=64)
+                hqs[i] = small.tile([P, NG, P], U8, name="hqs", align_bytes=64)
+            nc.vector.quantize_mx(
+                out=hq[i][:, g : g + n, :].rearrange("p c n -> p (c n)").bitcast(FP8X4),
+                scales=hqs[i][:, g : g + n, :].rearrange("p c n -> p (c n)"),
+                in_=pr[i, g][:].rearrange("p c n t -> p (c n t)"),
+            )
+
+        def mm1(i, g):
+            if i >= NT:
+                return
+            if g == 0:
+                kv[i] = ps_kv.tile([P, LAT], F32, name="kv")
+                rp[i] = ps_r.tile([P, ROPE], F32, name="rp")
+            for dst, c0, c1 in ((kv[i], 0, LAT), (rp[i], LAT, LAT + ROPE)):
+                nc.tensor.matmul_mx(
+                    out=dst[:],
+                    lhsT=hq[i][:, g, :].bitcast(FP8X4),
+                    lhsT_scale=hqs[i][:, g, :],
+                    rhs=wa[g][:, c0:c1].bitcast(FP8X4),
+                    rhs_scale=wa_s[4 * g :, c0:c1],
+                    start=(g == 0),
+                    stop=(g == NG - 1),
+                )
+
+        kt = [outs.tile([P, HEADS, HEAD], F32, name="kt%d" % i, bufs=1) for i in range(NT)]
+        vt = [outs.tile([P, HEADS, VD], F32, name="vt%d" % i, bufs=1) for i in range(NT)]
+
+        def rope(i):
+            xr = small.tile([P, ROPE // 2, 2], F32, name="xr")
+            nc.scalar.copy(out=xr[:].rearrange("p f e -> p (f e)"), in_=rp[i][:])
+            xc = small.tile([P, ROPE // 2, 2], F32, name="xc")
+            xs = small.tile([P, ROPE // 2, 2], F32, name="xs")
+            r = small.tile([P, ROPE // 2, 2], F32, name="r")
+            wide = [P, ROPE // 2, 2]
+            nc.gpsimd.tensor_tensor(out=xc[:], in0=xr[:], in1=cos_t[:, i, :].unsqueeze(2).to_broadcast(wide), op=ALU.mult)
+            nc.gpsimd.tensor_tensor(out=xs[:], in0=xr[:], in1=sin_t[:, i, :].unsqueeze(2).to_broadcast(wide), op=ALU.mult)
+            nc.gpsimd.tensor_tensor(out=r[:, :, 0], in0=xc[:, :, 0], in1=xs[:, :, 1], op=ALU.subtract)
+            nc.gpsimd.tensor_tensor(out=r[:, :, 1], in0=xs[:, :, 0], in1=xc[:, :, 1], op=ALU.add)
+            flat = r[:].rearrange("p f e -> p (f e)").unsqueeze(1).to_broadcast([P, 4, ROPE])
+            for h in range(0, HEADS, 4):
+                nc.gpsimd.tensor_scalar(
+                    out=kt[i][:, h : h + 4, NOPE:], in0=flat, scalar1=1.0, scalar2=0.0, op0=ALU.mult, op1=ALU.add
+                )
+
+        def stats(i):
+            st = small.tile([P, 6], F32, name="st")
+            nc.vector.bn_stats(out=st[:], in_=kv[i][:])
+            return st
+
+        def aggr(i, st):
+            mv[i] = small.tile([P, 2], F32, name="mv")
+            nc.vector.bn_aggr(out=mv[i][:], in_=st[:])
+            rs[i] = small.tile([P, 1], F32, name="rs")
+            nc.scalar.activation(out=rs[i][:], in_=mv[i][:, 1:2], func=ACT.Abs_reciprocal_sqrt, bias=EPS)
+
+        def norm1(i):
+            y1[i] = small.tile([P, LAT], F32, name="y1")
+            nc.vector.scalar_tensor_tensor(
+                out=y1[i][:], in0=kv[i][:], scalar=mv[i][:, 0:1], in1=gam[:], op0=ALU.subtract, op1=ALU.mult
+            )
+
+        def norm2(i):
+            lat[i] = small.tile([P, LAT], BF16, name="lat")
+            nc.vector.scalar_tensor_tensor(
+                out=lat[i][:], in0=y1[i][:], scalar=rs[i][:], in1=bet[:], op0=ALU.mult, op1=ALU.add
+            )
+
+        def lat_turn(i):
+            lt[i] = ps_x.tile([P, 2, P], F32, name="lt", tag="xt")
+            words = lat[i][:].bitcast(F32)
+            for j in range(2):
+                nc.tensor.transpose(lt[i][:, j, :], words[:, j : LAT // 2 : 2], ident32[:])
+
+        def lat_copy(i):
+            lg[i] = small.tile([P, P, 2], F32, name="lg", align_bytes=64)
+            nc.scalar.copy(out=lg[i][:], in_=lt[i][:].rearrange("p t n -> p n t"))
+
+        def lat_quant(i):
+            lq[i] = small.tile([P, P], U32, name="lq", align_bytes=64)
+            lqs[i] = small.tile([P, P], U8, name="lqs", align_bytes=64)
+            nc.vector.quantize_mx(out=lq[i][:].bitcast(FP8X4), scales=lqs[i][:], in_=lg[i][:].rearrange("p n t -> p (n t)").bitcast(BF16))
+
+        def mm2(i, out, c0, n):
+            nc.tensor.matmul_mx(
+                out=out,
+                lhsT=lq[i][:].bitcast(FP8X4),
+                lhsT_scale=lqs[i][:],
+                rhs=wb[:, c0 : c0 + n].bitcast(FP8X4),
+                rhs_scale=wb_s[:, c0 : c0 + n],
+                start=True,
+                stop=True,
+            )
+
+        ob = {}
+
+        def v_mm(i, b):
+            ob[i, "v", b] = ps_o.tile([P, 4, VD], F32, name="o", tag="o")
+            for j in range(4):
+                mm2(i, ob[i, "v", b][:, j, :], HEAD * (4 * b + j) + NOPE, VD)
+
+        def v_out(i, b, eng=None):
+            dst = vt[i][:, 4 * b : 4 * b + 4, :]
+            if eng is None:
+                nc.scalar.copy(out=dst, in_=ob[i, "v", b][:])
+            else:
+                eng.tensor_copy(out=dst, in_=ob[i, "v", b][:])
+
+        def k_mm(i, b):
+            ob[i, "k", b] = ps_o.tile([P, 8, NOPE], F32, name="o", tag="o")
+            for j in range(8):
+                mm2(i, ob[i, "k", b][:, j, :], HEAD * (8 * b + j), NOPE)
+
+        def k_out(i, b):
+            nc.scalar.copy(out=kt[i][:, 8 * b : 8 * b + 8, 0:NOPE], in_=ob[i, "k", b][:])
+
+        def store(dst, t, i, h0, h1):
+            nc.sync.dma_start(out=dst[0, i * P : (i + 1) * P, h0:h1, :], in_=t[i][:, h0:h1, :])
+
+        widen(0, 0, 1, nc.vector)
+        widen(0, 1)
+        widen(0, 2, 1, nc.vector)
+        widen(0, 3)
+        turn(0, 0)
+        scale(0, 0)
+        turn(0, 1)
+        scale(0, 1)
+        turn(0, 2)
+        quant(0, 0)
+        mm1(0, 0)
+        scale(0, 2)
+        turn(0, 3)
+        quant(0, 1)
+        mm1(0, 1)
+        scale(0, 3)
+        for g in range(NG):
+            widen(1, g)
+        turn(1, 0)
+        turn(1, 1)
+        quant(0, 2)
+        quant(0, 3)
+        mm1(0, 2)
+        mm1(0, 3)
+        scale(1, 0)
+        scale(1, 1)
+
+        lo = {1: ((0, 1), (1, 1)), 2: ((0, 2),), 3: ((0, 2),), 4: (), 5: ()}
+        hi = {1: ((2, 1), (3, 1)), 2: ((2, 2),), 3: ((2, 2),), 4: (), 5: ()}
+        for i in range(NT):
+            j, k = i + 1, i + 2
+            st = stats(i)
+            for c in lo[j][:1]:
+                quant(j, *c)
+            rope(i)
+            aggr(i, st)
+            for c in lo[j][1:]:
+                quant(j, *c)
+            norm1(i)
+            norm2(i)
+            if i == 0:
+                widen(2, 0, 2)
+                widen(2, 2, 2)
+            else:
+                v_out(i - 1, 2)
+                k_out(i - 1, 1)
+                store(out_k, kt, i - 1, 8, 16)
+            for c in hi[j]:
+                turn(j, *c)
+            lat_turn(i)
+            mm1(j, 0)
+            mm1(j, 1)
+            for c in hi[j]:
+                scale(j, *c)
+            lat_copy(i)
+            if i < 2:
+                widen(3, 2 * i, 2)
+            if i > 0:
+                v_out(i - 1, 3)
+                store(out_v, vt, i - 1, 8, 16)
+            lat_quant(i)
+            for c in lo[k]:
+                turn(k, *c)
+            for c in hi[j]:
+                quant(j, *c)
+            v_mm(i, 0)
+            v_out(i, 0)
+            if i == 0:
+                store(out_v, vt, i, 0, 4)
+            v_mm(i, 1)
+            v_out(i, 1, nc.vector if i == NT - 1 else None)
+            store(out_v, vt, i, 4 if i == 0 else 0, 8)
+            mm1(j, 2)
+            mm1(j, 3)
+            k_mm(i, 0)
+            k_out(i, 0)
+            store(out_k, kt, i, 0, 8)
+            for c in lo[k]:
+                scale(k, *c)
+            v_mm(i, 2)
+            k_mm(i, 1)
+            v_mm(i, 3)
+        i = NT - 1
+        v_out(i, 2)
+        k_out(i, 1)
+        store(out_k, kt, i, 8, 16)
+        v_out(i, 3, nc.vector)
+        store(out_v, vt, i, 8, 16)

@@ -48,10 +48,23 @@ def tile_multilatentattention_pa_w8_kernel(
         wb_s = keep.tile([P, HEADS * HEAD], U8, name="wb_s", align_bytes=64)
         nc.vector.memset(wa_s[:].bitcast(I32), 0)
         nc.vector.memset(wb_s[:].bitcast(I32), 0)
+        ones = keep.tile([P, P], BF16, name="ones")
+        nc.gpsimd.memset(ones[:], 1.0)
+        zeros = keep.tile([P, LAT], BF16, name="zeros")
+        nc.gpsimd.memset(zeros[:].bitcast(I32), 0)
+        gb_row = keep.tile([P, 2, LAT], BF16, name="gb_row")
         ident32 = keep.tile([P, P], F32, name="ident32")
         make_identity(nc, ident32[:])
         ident = keep.tile([P, P], BF16, name="ident")
         nc.vector.tensor_copy(out=ident[:], in_=ident32[:])
+        nc.gpsimd.memset(gb_row[:].bitcast(I32), 0)
+
+        def warm_up(n):
+            w = ps_o.tile([P, LAT], F32, name="o", tag="o")
+            for w_i in range(n):
+                nc.tensor.matmul(out=w[:], lhsT=ones[:], rhs=zeros[:], start=True, stop=True)
+
+        warm_up(4)
 
         hb = [keep.tile([P, HID], U8, name="hb%d" % i) for i in range(NT)]
         wa = [keep.tile([P, LAT + ROPE], U32, name="wa%d" % g, align_bytes=64) for g in range(NG)]
@@ -59,11 +72,15 @@ def tile_multilatentattention_pa_w8_kernel(
         hs = keep.tile([P, NG, PACK], F32, name="hs")
         cos_t = keep.tile([P, NT, ROPE // 2], BF16, name="cos_t")
         sin_t = keep.tile([P, NT, ROPE // 2], BF16, name="sin_t")
-        gam = keep.tile([P, LAT], BF16, name="gam")
-        bet = keep.tile([P, LAT], BF16, name="bet")
+        gb = keep.tile([P, 2, LAT], BF16, name="gb")
+        gam, bet = gb[:, 0, :], gb[:, 1, :]
+
+        h_rows = h_bytes[0].rearrange("(p i) k -> p i k", i=NT)
+        k_rows = out_k[0].rearrange("(p i) h d -> p i h d", i=NT)
+        v_rows = out_v[0].rearrange("(p i) h d -> p i h d", i=NT)
 
         def load_h(i):
-            nc.sync.dma_start(out=hb[i][:], in_=h_bytes[0, i * P : (i + 1) * P, :])
+            nc.sync.dma_start(out=hb[i][:], in_=h_rows[:, i, :])
 
         def load_wa(g):
             nc.sync.dma_start(out=wa[g][:].bitcast(I32), in_=wa_words[g].rearrange("p n t -> p (n t)").bitcast(I32))
@@ -77,8 +94,8 @@ def tile_multilatentattention_pa_w8_kernel(
         load_h(1)
         load_wa(2)
         load_wa(3)
-        nc.sync.dma_start(out=gam[:], in_=gamma.partition_broadcast(P))
-        nc.sync.dma_start(out=bet[:], in_=beta.partition_broadcast(P))
+        nc.sync.dma_start(out=gb_row[0:1, 0, :], in_=gamma.unsqueeze(0))
+        nc.sync.dma_start(out=gb_row[0:1, 1, :], in_=beta.unsqueeze(0))
         wb_flat = wb_words[0].rearrange("p n t -> p (n t)").bitcast(I32)
         half = HEADS * HEAD // 2
 
@@ -86,8 +103,8 @@ def tile_multilatentattention_pa_w8_kernel(
             nc.sync.dma_start(out=wb[:, j * half : (j + 1) * half].bitcast(I32), in_=wb_flat[:, j * half : (j + 1) * half])
 
         load_wb(0)
-        nc.sync.dma_start(out=cos_t[:], in_=cos.rearrange("(i p) f -> p i f", p=P))
-        nc.sync.dma_start(out=sin_t[:], in_=sin.rearrange("(i p) f -> p i f", p=P))
+        nc.sync.dma_start(out=cos_t[:], in_=cos.rearrange("(p i) f -> p i f", i=NT))
+        nc.sync.dma_start(out=sin_t[:], in_=sin.rearrange("(p i) f -> p i f", i=NT))
         for q in range(4):
             nc.sync.dma_start(out=wb_s[32 * q : 32 * q + 4, :].bitcast(I32), in_=wb_scales[0, 4 * q : 4 * q + 4, :].bitcast(I32))
         load_h(2)
@@ -159,7 +176,7 @@ def tile_multilatentattention_pa_w8_kernel(
                     stop=(g == NG - 1),
                 )
 
-        kt = [outs.tile([P, HEADS, HEAD], F32, name="kt%d" % i, bufs=1) for i in range(NT)]
+        kt = [outs.tile([P, HEADS, HEAD if i else NOPE], F32, name="kt%d" % i, bufs=1) for i in range(NT)]
         vt = [outs.tile([P, HEADS, VD], F32, name="vt%d" % i, bufs=1) for i in range(NT)]
 
         def rope(i):
@@ -173,6 +190,10 @@ def tile_multilatentattention_pa_w8_kernel(
             nc.gpsimd.tensor_tensor(out=xs[:], in0=xr[:], in1=sin_t[:, i, :].unsqueeze(2).to_broadcast(wide), op=ALU.mult)
             nc.gpsimd.tensor_tensor(out=r[:, :, 0], in0=xc[:, :, 0], in1=xs[:, :, 1], op=ALU.subtract)
             nc.gpsimd.tensor_tensor(out=r[:, :, 1], in0=xs[:, :, 0], in1=xc[:, :, 1], op=ALU.add)
+            if i == 0:
+                flat = r[:].rearrange("p f e -> p (f e)").unsqueeze(1).to_broadcast([P, HEADS, ROPE])
+                nc.sync.dma_start(out=k_rows[:, i, :, NOPE:], in_=flat)
+                return
             flat = r[:].rearrange("p f e -> p (f e)").unsqueeze(1).to_broadcast([P, 4, ROPE])
             for h in range(0, HEADS, 4):
                 nc.gpsimd.tensor_scalar(
@@ -193,13 +214,13 @@ def tile_multilatentattention_pa_w8_kernel(
         def norm1(i):
             y1[i] = small.tile([P, LAT], F32, name="y1")
             nc.vector.scalar_tensor_tensor(
-                out=y1[i][:], in0=kv[i][:], scalar=mv[i][:, 0:1], in1=gam[:], op0=ALU.subtract, op1=ALU.mult
+                out=y1[i][:], in0=kv[i][:], scalar=mv[i][:, 0:1], in1=gam, op0=ALU.subtract, op1=ALU.mult
             )
 
         def norm2(i):
             lat[i] = small.tile([P, LAT], BF16, name="lat")
             nc.vector.scalar_tensor_tensor(
-                out=lat[i][:], in0=y1[i][:], scalar=rs[i][:], in1=bet[:], op0=ALU.mult, op1=ALU.add
+                out=lat[i][:], in0=y1[i][:], scalar=rs[i][:], in1=bet, op0=ALU.mult, op1=ALU.add
             )
 
         def lat_turn(i):
@@ -251,7 +272,8 @@ def tile_multilatentattention_pa_w8_kernel(
             nc.scalar.copy(out=kt[i][:, 8 * b : 8 * b + 8, 0:NOPE], in_=ob[i, "k", b][:])
 
         def store(dst, t, i, h0, h1):
-            nc.sync.dma_start(out=dst[0, i * P : (i + 1) * P, h0:h1, :], in_=t[i][:, h0:h1, :])
+            d = t[i].shape[-1]
+            nc.sync.dma_start(out=dst[:, i, h0:h1, 0:d], in_=t[i][:, h0:h1, :])
 
         widen(0, 0, 1, nc.vector)
         widen(0, 1)
@@ -260,6 +282,7 @@ def tile_multilatentattention_pa_w8_kernel(
         turn(0, 0)
         scale(0, 0)
         turn(0, 1)
+        warm_up(2)
         scale(0, 1)
         turn(0, 2)
         quant(0, 0)
@@ -273,6 +296,10 @@ def tile_multilatentattention_pa_w8_kernel(
             widen(1, g)
         turn(1, 0)
         turn(1, 1)
+        for j in range(2):
+            g_ps = ps_o.tile([P, LAT], F32, name="o", tag="o")
+            nc.tensor.matmul(out=g_ps[:], lhsT=ones[:], rhs=gb_row[:, j, :], start=True, stop=True)
+            nc.scalar.copy(out=gb[:, j, :], in_=g_ps[:])
         quant(0, 2)
         quant(0, 3)
         mm1(0, 2)
@@ -299,9 +326,11 @@ def tile_multilatentattention_pa_w8_kernel(
             else:
                 v_out(i - 1, 2)
                 k_out(i - 1, 1)
-                store(out_k, kt, i - 1, 8, 16)
+                store(k_rows, kt, i - 1, 8, 16)
             for c in hi[j]:
                 turn(j, *c)
+            if i == 0:
+                warm_up(3)
             lat_turn(i)
             mm1(j, 0)
             mm1(j, 1)
@@ -312,7 +341,7 @@ def tile_multilatentattention_pa_w8_kernel(
                 widen(3, 2 * i, 2)
             if i > 0:
                 v_out(i - 1, 3)
-                store(out_v, vt, i - 1, 8, 16)
+                store(v_rows, vt, i - 1, 8, 16)
             lat_quant(i)
             for c in lo[k]:
                 turn(k, *c)
@@ -321,15 +350,15 @@ def tile_multilatentattention_pa_w8_kernel(
             v_mm(i, 0)
             v_out(i, 0)
             if i == 0:
-                store(out_v, vt, i, 0, 4)
+                store(v_rows, vt, i, 0, 4)
             v_mm(i, 1)
             v_out(i, 1, nc.vector if i == NT - 1 else None)
-            store(out_v, vt, i, 4 if i == 0 else 0, 8)
+            store(v_rows, vt, i, 4 if i == 0 else 0, 8)
             mm1(j, 2)
             mm1(j, 3)
             k_mm(i, 0)
             k_out(i, 0)
-            store(out_k, kt, i, 0, 8)
+            store(k_rows, kt, i, 0, 8)
             for c in lo[k]:
                 scale(k, *c)
             v_mm(i, 2)
@@ -338,6 +367,6 @@ def tile_multilatentattention_pa_w8_kernel(
         i = NT - 1
         v_out(i, 2)
         k_out(i, 1)
-        store(out_k, kt, i, 8, 16)
+        store(k_rows, kt, i, 8, 16)
         v_out(i, 3, nc.vector)
-        store(out_v, vt, i, 8, 16)
+        store(v_rows, vt, i, 8, 16)

@@ -117,7 +117,7 @@ def tile_multilatentattention_pa_w8_kernel(
         def widen(i, g, n=1, eng=None):
             if i >= NT:
                 return
-            x = stage.tile([P, n * KP], BF16, name="xw%d" % n, bufs=8 if n == 1 else 4)
+            x = stage.tile([P, n * KP], BF16, name="xw%d" % n, bufs=16)
             for j in range(n):
                 xw[i, g + j] = x[:, j * KP : (j + 1) * KP]
             src = hb[i][:, g * KP : (g + n) * KP].bitcast(FP8)
@@ -250,34 +250,49 @@ def tile_multilatentattention_pa_w8_kernel(
             )
 
         ob = {}
+        banks = (("k", 0), ("v", 0), ("k", 1), ("v", 1), ("v", 2), ("v", 3))
 
-        def v_mm(i, b):
-            ob[i, "v", b] = ps_o.tile([P, 4, VD], F32, name="o", tag="o")
-            for j in range(4):
-                mm2(i, ob[i, "v", b][:, j, :], HEAD * (4 * b + j) + NOPE, VD)
-
-        def v_out(i, b, eng=None):
-            dst = vt[i][:, 4 * b : 4 * b + 4, :]
-            if eng is None:
-                nc.scalar.copy(out=dst, in_=ob[i, "v", b][:])
+        def up(i, b):
+            kind, n = banks[b]
+            o = ps_o.tile([P, LAT], F32, name="o", tag="o")
+            ob[i, b] = o
+            if kind == "v":
+                for j in range(4):
+                    mm2(i, o[:, j * VD : (j + 1) * VD], HEAD * (4 * n + j) + NOPE, VD)
             else:
-                eng.tensor_copy(out=dst, in_=ob[i, "v", b][:])
+                for j in range(8):
+                    mm2(i, o[:, j * NOPE : (j + 1) * NOPE], HEAD * (8 * n + j), NOPE)
 
-        def k_mm(i, b):
-            ob[i, "k", b] = ps_o.tile([P, 8, NOPE], F32, name="o", tag="o")
-            for j in range(8):
-                mm2(i, ob[i, "k", b][:, j, :], HEAD * (8 * b + j), NOPE)
-
-        def k_out(i, b):
-            nc.scalar.copy(out=kt[i][:, 8 * b : 8 * b + 8, 0:NOPE], in_=ob[i, "k", b][:])
+        def out(i, b, eng=None):
+            kind, n = banks[b]
+            if kind == "v":
+                dst = vt[i][:, 4 * n : 4 * n + 4, :]
+                src = ob[i, b][:].rearrange("p (h d) -> p h d", d=VD)
+            else:
+                dst = kt[i][:, 8 * n : 8 * n + 8, 0:NOPE]
+                src = ob[i, b][:].rearrange("p (h d) -> p h d", d=NOPE)
+            if eng is None:
+                nc.scalar.copy(out=dst, in_=src)
+            else:
+                eng.tensor_copy(out=dst, in_=src)
+            if b == 0 and i > 0:
+                store(k_rows, kt, i, 0, 8)
+            if b == 1 and i == 0:
+                store(v_rows, vt, i, 0, 4)
+            if b == 2:
+                store(k_rows, kt, i, 8 if i else 0, 16)
+            if b == 3:
+                store(v_rows, vt, i, 0 if i else 4, 8)
+            if b == (5 if i in (0, NT - 1) else 4):
+                store(v_rows, vt, i, 8, 16)
 
         def store(dst, t, i, h0, h1):
             d = t[i].shape[-1]
             nc.sync.dma_start(out=dst[:, i, h0:h1, 0:d], in_=t[i][:, h0:h1, :])
 
         widen(0, 0, 1, nc.vector)
-        widen(0, 1)
-        widen(0, 2, 1, nc.vector)
+        widen(0, 1, 1, nc.vector)
+        widen(0, 2)
         widen(0, 3)
         turn(0, 0)
         scale(0, 0)
@@ -285,88 +300,94 @@ def tile_multilatentattention_pa_w8_kernel(
         warm_up(2)
         scale(0, 1)
         turn(0, 2)
-        quant(0, 0)
-        mm1(0, 0)
         scale(0, 2)
+        quant(0, 0)
         turn(0, 3)
-        quant(0, 1)
-        mm1(0, 1)
         scale(0, 3)
+        for g in range(1, NG):
+            quant(0, g)
         for g in range(NG):
             widen(1, g)
         turn(1, 0)
+        mm1(0, 0)
         turn(1, 1)
+        mm1(0, 1)
         for j in range(2):
             g_ps = ps_o.tile([P, LAT], F32, name="o", tag="o")
             nc.tensor.matmul(out=g_ps[:], lhsT=ones[:], rhs=gb_row[:, j, :], start=True, stop=True)
             nc.scalar.copy(out=gb[:, j, :], in_=g_ps[:])
-        quant(0, 2)
-        quant(0, 3)
+        for g in range(3):
+            widen(2, g)
+        turn(1, 2)
         mm1(0, 2)
         mm1(0, 3)
         scale(1, 0)
+        turn(1, 3)
         scale(1, 1)
+        turn(2, 0)
+        quant(1, 0)
+        scale(1, 2)
+        turn(2, 1)
+        warm_up(2)
+        rope(0)
 
-        lo = {1: ((0, 1), (1, 1)), 2: ((0, 2),), 3: ((0, 2),), 4: (), 5: ()}
-        hi = {1: ((2, 1), (3, 1)), 2: ((2, 2),), 3: ((2, 2),), 4: (), 5: ()}
         for i in range(NT):
-            j, k = i + 1, i + 2
+            h, j, k, l = i - 1, i + 1, i + 2, i + 3
             st = stats(i)
-            for c in lo[j][:1]:
-                quant(j, *c)
-            rope(i)
+            quant(j, 1)
             aggr(i, st)
-            for c in lo[j][1:]:
-                quant(j, *c)
-            norm1(i)
-            norm2(i)
+            quant(j, 2)
             if i == 0:
-                widen(2, 0, 2)
-                widen(2, 2, 2)
+                for g in range(3):
+                    widen(3, g)
             else:
-                v_out(i - 1, 2)
-                k_out(i - 1, 1)
-                store(k_rows, kt, i - 1, 8, 16)
-            for c in hi[j]:
-                turn(j, *c)
-            if i == 0:
-                warm_up(3)
-            lat_turn(i)
+                out(h, 2)
+                out(h, 3)
+            norm1(i)
+            if i > 0:
+                up(h, 4)
+            if i == 1:
+                out(h, 4)
             mm1(j, 0)
             mm1(j, 1)
-            for c in hi[j]:
-                scale(j, *c)
-            lat_copy(i)
-            if i < 2:
-                widen(3, 2 * i, 2)
+            scale(j, 3)
+            norm2(i)
+            lat_turn(i)
             if i > 0:
-                v_out(i - 1, 3)
-                store(v_rows, vt, i - 1, 8, 16)
-            lat_quant(i)
-            for c in lo[k]:
-                turn(k, *c)
-            for c in hi[j]:
-                quant(j, *c)
-            v_mm(i, 0)
-            v_out(i, 0)
+                up(h, 5)
+            lat_copy(i)
             if i == 0:
-                store(v_rows, vt, i, 0, 4)
-            v_mm(i, 1)
-            v_out(i, 1, nc.vector if i == NT - 1 else None)
-            store(v_rows, vt, i, 4 if i == 0 else 0, 8)
+                widen(2, 3)
+            else:
+                out(h, 5)
+            if i == 1:
+                widen(3, 3)
+            scale(k, 0)
+            quant(j, 3)
+            quant(k, 0)
+            scale(k, 1)
+            lat_quant(i)
+            turn(k, 2)
             mm1(j, 2)
             mm1(j, 3)
-            k_mm(i, 0)
-            k_out(i, 0)
-            store(k_rows, kt, i, 0, 8)
-            for c in lo[k]:
-                scale(k, *c)
-            v_mm(i, 2)
-            k_mm(i, 1)
-            v_mm(i, 3)
+            if j < NT:
+                rope(j)
+            up(i, 0)
+            out(i, 0)
+            scale(k, 2)
+            if h > 0:
+                out(h, 4, nc.vector)
+            up(i, 1)
+            out(i, 1)
+            up(i, 2)
+            turn(k, 3)
+            turn(l, 0)
+            up(i, 3)
+            turn(l, 1)
         i = NT - 1
-        v_out(i, 2)
-        k_out(i, 1)
-        store(k_rows, kt, i, 8, 16)
-        v_out(i, 3, nc.vector)
-        store(v_rows, vt, i, 8, 16)
+        out(i, 3, nc.vector)
+        out(i, 2)
+        up(i, 4)
+        out(i, 4, nc.vector)
+        up(i, 5)
+        out(i, 5)

@@ -24,6 +24,7 @@ PACK = 4
 KP = P * PACK
 NG = HID // KP
 NT = T // P
+DIRECT = (0,)
 
 
 def tile_multilatentattention_pa_w8_kernel(
@@ -96,20 +97,29 @@ def tile_multilatentattention_pa_w8_kernel(
         load_wa(3)
         nc.sync.dma_start(out=gb_row[0:1, 0, :], in_=gamma.unsqueeze(0))
         nc.sync.dma_start(out=gb_row[0:1, 1, :], in_=beta.unsqueeze(0))
-        wb_flat = wb_words[0].rearrange("p n t -> p (n t)").bitcast(I32)
-        half = HEADS * HEAD // 2
-
-        def load_wb(j):
-            nc.sync.dma_start(out=wb[:, j * half : (j + 1) * half].bitcast(I32), in_=wb_flat[:, j * half : (j + 1) * half])
-
-        load_wb(0)
         nc.sync.dma_start(out=cos_t[:], in_=cos.rearrange("(p i) f -> p i f", i=NT))
         nc.sync.dma_start(out=sin_t[:], in_=sin.rearrange("(p i) f -> p i f", i=NT))
-        for q in range(4):
-            nc.sync.dma_start(out=wb_s[32 * q : 32 * q + 4, :].bitcast(I32), in_=wb_scales[0, 4 * q : 4 * q + 4, :].bitcast(I32))
         load_h(2)
-        load_wb(1)
+        wb_heads = wb_words[0].rearrange("p n t -> p (n t)").bitcast(I32).rearrange("p (h c) -> p h c", c=HEAD)
+        wb_i32 = wb[:].bitcast(I32)
+        wbs_i32 = wb_s[:].bitcast(I32)
+        nn = HEADS * NOPE
+
+        def load_wb(h0, h1, c0, c1, at):
+            w = c1 - c0
+            nc.sync.dma_start(
+                out=wb_i32[:, at + h0 * w : at + h1 * w].rearrange("p (h c) -> p h c", c=w), in_=wb_heads[:, h0:h1, c0:c1]
+            )
+
+        load_wb(0, 16, 0, NOPE, 0)
+        load_wb(0, 8, NOPE, HEAD, nn)
+        for q in range(4):
+            src = wb_scales[0, 4 * q : 4 * q + 4, :].bitcast(I32).rearrange("q (h c) -> q h c", c=HEAD // 4)
+            rows = wbs_i32[32 * q : 32 * q + 4, :]
+            nc.sync.dma_start(out=rows[:, 0 : nn // 4].rearrange("q (h c) -> q h c", c=NOPE // 4), in_=src[:, :, 0 : NOPE // 4])
+            nc.sync.dma_start(out=rows[:, nn // 4 :].rearrange("q (h c) -> q h c", c=VD // 4), in_=src[:, :, NOPE // 4 :])
         load_h(3)
+        load_wb(8, 16, NOPE, HEAD, nn)
 
         xw, xt, pr, hq, hqs, kv, rp = {}, {}, {}, {}, {}, {}, {}
         mv, rs, y1, lat, lt, lg, lq, lqs = {}, {}, {}, {}, {}, {}, {}, {}
@@ -176,7 +186,7 @@ def tile_multilatentattention_pa_w8_kernel(
                     stop=(g == NG - 1),
                 )
 
-        kt = [outs.tile([P, HEADS, HEAD if i else NOPE], F32, name="kt%d" % i, bufs=1) for i in range(NT)]
+        kt = [outs.tile([P, HEADS, NOPE if i in DIRECT else HEAD], F32, name="kt%d" % i, bufs=1) for i in range(NT)]
         vt = [outs.tile([P, HEADS, VD], F32, name="vt%d" % i, bufs=1) for i in range(NT)]
 
         def rope(i):
@@ -190,7 +200,7 @@ def tile_multilatentattention_pa_w8_kernel(
             nc.gpsimd.tensor_tensor(out=xs[:], in0=xr[:], in1=sin_t[:, i, :].unsqueeze(2).to_broadcast(wide), op=ALU.mult)
             nc.gpsimd.tensor_tensor(out=r[:, :, 0], in0=xc[:, :, 0], in1=xs[:, :, 1], op=ALU.subtract)
             nc.gpsimd.tensor_tensor(out=r[:, :, 1], in0=xs[:, :, 0], in1=xc[:, :, 1], op=ALU.add)
-            if i == 0:
+            if i in DIRECT:
                 flat = r[:].rearrange("p f e -> p (f e)").unsqueeze(1).to_broadcast([P, HEADS, ROPE])
                 nc.sync.dma_start(out=k_rows[:, i, :, NOPE:], in_=flat)
                 return
@@ -256,12 +266,7 @@ def tile_multilatentattention_pa_w8_kernel(
             kind, n = banks[b]
             o = ps_o.tile([P, LAT], F32, name="o", tag="o")
             ob[i, b] = o
-            if kind == "v":
-                for j in range(4):
-                    mm2(i, o[:, j * VD : (j + 1) * VD], HEAD * (4 * n + j) + NOPE, VD)
-            else:
-                for j in range(8):
-                    mm2(i, o[:, j * NOPE : (j + 1) * NOPE], HEAD * (8 * n + j), NOPE)
+            mm2(i, o[:], 512 * n + (nn if kind == "v" else 0), 512)
 
         def out(i, b, eng=None):
             kind, n = banks[b]
@@ -275,12 +280,12 @@ def tile_multilatentattention_pa_w8_kernel(
                 nc.scalar.copy(out=dst, in_=src)
             else:
                 eng.tensor_copy(out=dst, in_=src)
-            if b == 0 and i > 0:
+            if b == 0 and i == 3:
                 store(k_rows, kt, i, 0, 8)
             if b == 1 and i == 0:
                 store(v_rows, vt, i, 0, 4)
             if b == 2:
-                store(k_rows, kt, i, 8 if i else 0, 16)
+                store(k_rows, kt, i, 8 if i == 3 else 0, 16)
             if b == 3:
                 store(v_rows, vt, i, 0 if i else 4, 8)
             if b == (5 if i in (0, NT - 1) else 4):
@@ -316,11 +321,13 @@ def tile_multilatentattention_pa_w8_kernel(
             g_ps = ps_o.tile([P, LAT], F32, name="o", tag="o")
             nc.tensor.matmul(out=g_ps[:], lhsT=ones[:], rhs=gb_row[:, j, :], start=True, stop=True)
             nc.scalar.copy(out=gb[:, j, :], in_=g_ps[:])
-        for g in range(3):
-            widen(2, g)
+        widen(2, 0)
         turn(1, 2)
         mm1(0, 2)
         mm1(0, 3)
+        rope(0)
+        widen(2, 1)
+        widen(2, 2)
         scale(1, 0)
         turn(1, 3)
         scale(1, 1)
@@ -329,7 +336,6 @@ def tile_multilatentattention_pa_w8_kernel(
         scale(1, 2)
         turn(2, 1)
         warm_up(2)
-        rope(0)
 
         for i in range(NT):
             h, j, k, l = i - 1, i + 1, i + 2, i + 3
@@ -338,36 +344,37 @@ def tile_multilatentattention_pa_w8_kernel(
             aggr(i, st)
             quant(j, 2)
             if i == 0:
-                for g in range(3):
-                    widen(3, g)
+                widen(2, 3)
+                widen(3, 0)
             else:
                 out(h, 2)
                 out(h, 3)
             norm1(i)
+            mm1(j, 0)
+            mm1(j, 1)
             if i > 0:
                 up(h, 4)
             if i == 1:
                 out(h, 4)
-            mm1(j, 0)
-            mm1(j, 1)
             scale(j, 3)
             norm2(i)
             lat_turn(i)
+            lat_copy(i)
+            scale(k, 0)
+            turn(k, 2)
             if i > 0:
                 up(h, 5)
-            lat_copy(i)
             if i == 0:
-                widen(2, 3)
+                widen(3, 1)
+                widen(3, 2)
             else:
                 out(h, 5)
             if i == 1:
                 widen(3, 3)
-            scale(k, 0)
             quant(j, 3)
             quant(k, 0)
             scale(k, 1)
             lat_quant(i)
-            turn(k, 2)
             mm1(j, 2)
             mm1(j, 3)
             if j < NT:
@@ -382,8 +389,8 @@ def tile_multilatentattention_pa_w8_kernel(
             up(i, 2)
             turn(k, 3)
             turn(l, 0)
-            up(i, 3)
             turn(l, 1)
+            up(i, 3)
         i = NT - 1
         out(i, 3, nc.vector)
         out(i, 2)

@@ -280,12 +280,12 @@ def tile_multilatentattention_pa_w8_kernel(
                 nc.scalar.copy(out=dst, in_=src)
             else:
                 eng.tensor_copy(out=dst, in_=src)
-            if b == 0 and i == 3:
+            if b == 0 and i > 0:
                 store(k_rows, kt, i, 0, 8)
             if b == 1 and i == 0:
                 store(v_rows, vt, i, 0, 4)
             if b == 2:
-                store(k_rows, kt, i, 8 if i == 3 else 0, 16)
+                store(k_rows, kt, i, 8 if i > 0 else 0, 16)
             if b == 3:
                 store(v_rows, vt, i, 0 if i else 4, 8)
             if b == (5 if i in (0, NT - 1) else 4):

from contextlib import ExitStack

import concourse.mybir as mybir
from concourse.masks import make_identity

T, HID, LAT, ROPE = 512, 2048, 512, 128
HEADS, NOPE, VD = 16, 64, 128
HEAD = NOPE + VD
EPS = 1e-5
FLOPS = 2 * T * HID * (LAT + ROPE) + 2 * T * LAT * HEADS * HEAD

F32 = mybir.dt.float32
BF16 = mybir.dt.bfloat16
I32 = mybir.dt.int32
U32 = mybir.dt.uint32
U8 = mybir.dt.uint8
FP8 = mybir.dt.float8_e4m3fn
FP8X4 = mybir.dt.float8_e4m3fn_x4
ACT = mybir.ActivationFunctionType
ALU = mybir.AluOpType

P = 128
PACK = 4
KP = P * PACK
NG = HID // KP
NT = T // P
DIRECT = (0,)


def tile_multilatentattention_pa_w8_kernel(
    tc, h_bytes, h_scale, cos, sin, wa_words, wa_scales, gamma, beta, wb_words, wb_scales, out_k, out_v
):
    nc = tc.nc
    with ExitStack() as ctx:
        keep = ctx.enter_context(tc.tile_pool(name="keep", bufs=1))
        stage = ctx.enter_context(tc.tile_pool(name="stage", bufs=4))
        small = ctx.enter_context(tc.tile_pool(name="small", bufs=2))
        outs = ctx.enter_context(tc.tile_pool(name="outs", bufs=4))
        ps_x = ctx.enter_context(tc.psum_pool(name="ps_x", bufs=3))
        ps_kv = ctx.enter_context(tc.psum_pool(name="ps_kv", bufs=1))
        ps_r = ctx.enter_context(tc.psum_pool(name="ps_r", bufs=1))
        ps_o = ctx.enter_context(tc.psum_pool(name="ps_o", bufs=3))
        ctx.enter_context(tc.manual_schedule())

        warm = keep.tile([P, 1], F32, name="warm")
        nc.vector.memset(warm[:], 1.0)
        nc.scalar.activation(out=warm[:], in_=warm[:], func=ACT.Abs_reciprocal_sqrt)
        wa_s = keep.tile([P, LAT + ROPE], U8, name="wa_s", align_bytes=64)
        wb_s = keep.tile([P, HEADS * HEAD], U8, name="wb_s", align_bytes=64)
        nc.vector.memset(wa_s[:].bitcast(I32), 0)
        nc.vector.memset(wb_s[:].bitcast(I32), 0)
        ones = keep.tile([P, P], BF16, name="ones")
        nc.gpsimd.memset(ones[:], 1.0)
        zeros = keep.tile([P, LAT], BF16, name="zeros")
        nc.gpsimd.memset(zeros[:].bitcast(I32), 0)
        gb_row = keep.tile([P, 2, LAT], BF16, name="gb_row")
        ident32 = keep.tile([P, P], F32, name="ident32")
        make_identity(nc, ident32[:])
        ident = keep.tile([P, P], BF16, name="ident")
        nc.vector.tensor_copy(out=ident[:], in_=ident32[:])
        nc.gpsimd.memset(gb_row[:].bitcast(I32), 0)

        def warm_up(n):
            w = ps_o.tile([P, LAT], F32, name="o", tag="o")
            for w_i in range(n):
                nc.tensor.matmul(out=w[:], lhsT=ones[:], rhs=zeros[:], start=True, stop=True)

        warm_up(4)

        hb = [keep.tile([P, HID], U8, name="hb%d" % i) for i in range(NT)]
        wa = [keep.tile([P, LAT + ROPE], U32, name="wa%d" % g, align_bytes=64) for g in range(NG)]
        wb = keep.tile([P, HEADS * HEAD], U32, name="wb", align_bytes=64)
        hs = keep.tile([P, NG, PACK], F32, name="hs")
        cos_t = keep.tile([P, NT, ROPE // 2], BF16, name="cos_t")
        sin_t = keep.tile([P, NT, ROPE // 2], BF16, name="sin_t")
        gb = keep.tile([P, 2, LAT], BF16, name="gb")
        gam, bet = gb[:, 0, :], gb[:, 1, :]

        h_rows = h_bytes[0].rearrange("(p i) k -> p i k", i=NT)
        k_rows = out_k[0].rearrange("(p i) h d -> p i h d", i=NT)
        v_rows = out_v[0].rearrange("(p i) h d -> p i h d", i=NT)

        def load_h(i):
            nc.sync.dma_start(out=hb[i][:], in_=h_rows[:, i, :])

        def load_wa(g):
            nc.sync.dma_start(out=wa[g][:].bitcast(I32), in_=wa_words[g].rearrange("p n t -> p (n t)").bitcast(I32))

        load_h(0)
        nc.sync.dma_start(out=hs[:], in_=h_scale.rearrange("a b (g p t) -> p (a b g) t", p=P, t=PACK))
        for q in range(4):
            nc.sync.dma_start(out=wa_s[32 * q : 32 * q + 16, :].bitcast(I32), in_=wa_scales[:, 4 * q : 4 * q + 4, :].bitcast(I32))
        load_wa(0)
        load_wa(1)
        load_h(1)
        load_wa(2)
        load_wa(3)
        nc.sync.dma_start(out=gb_row[0:1, 0, :], in_=gamma.unsqueeze(0))
        nc.sync.dma_start(out=gb_row[0:1, 1, :], in_=beta.unsqueeze(0))
        nc.sync.dma_start(out=cos_t[:], in_=cos.rearrange("(p i) f -> p i f", i=NT))
        nc.sync.dma_start(out=sin_t[:], in_=sin.rearrange("(p i) f -> p i f", i=NT))
        load_h(2)
        wb_heads = wb_words[0].rearrange("p n t -> p (n t)").bitcast(I32).rearrange("p (h c) -> p h c", c=HEAD)
        wb_i32 = wb[:].bitcast(I32)
        wbs_i32 = wb_s[:].bitcast(I32)
        nn = HEADS * NOPE

        def load_wb(h0, h1, c0, c1, at):
            w = c1 - c0
            nc.sync.dma_start(
                out=wb_i32[:, at + h0 * w : at + h1 * w].rearrange("p (h c) -> p h c", c=w), in_=wb_heads[:, h0:h1, c0:c1]
            )

        load_wb(0, 16, 0, NOPE, 0)
        load_wb(0, 8, NOPE, HEAD, nn)
        for q in range(4):
            src = wb_scales[0, 4 * q : 4 * q + 4, :].bitcast(I32).rearrange("q (h c) -> q h c", c=HEAD // 4)
            rows = wbs_i32[32 * q : 32 * q + 4, :]
            nc.sync.dma_start(out=rows[:, 0 : nn // 4].rearrange("q (h c) -> q h c", c=NOPE // 4), in_=src[:, :, 0 : NOPE // 4])
            nc.sync.dma_start(out=rows[:, nn // 4 :].rearrange("q (h c) -> q h c", c=VD // 4), in_=src[:, :, NOPE // 4 :])
        load_h(3)
        load_wb(8, 16, NOPE, HEAD, nn)

        xw, xt, pr, hq, hqs, kv, rp = {}, {}, {}, {}, {}, {}, {}
        mv, rs, y1, lat, lt, lg, lq, lqs = {}, {}, {}, {}, {}, {}, {}, {}

        def widen(i, g, n=1, eng=None):
            if i >= NT:
                return
            x = stage.tile([P, n * KP], BF16, name="xw%d" % n, bufs=16)
            for j in range(n):
                xw[i, g + j] = x[:, j * KP : (j + 1) * KP]
            src = hb[i][:, g * KP : (g + n) * KP].bitcast(FP8)
            if eng is None:
                nc.scalar.copy(out=x[:], in_=src)
            else:
                eng.tensor_copy(out=x[:], in_=src)

        def turn(i, g, n=1):
            if i >= NT:
                return
            t = ps_x.tile([P, n, PACK, P], BF16, name="xt", tag="xt")
            xt[i, g] = t
            for c in range(n):
                for j in range(PACK):
                    nc.tensor.transpose(t[:, c, j, :], xw[i, g + c][:, j : KP : PACK], ident[:])

        def scale(i, g, n=1):
            if i >= NT:
                return
            p = stage.tile([P, n, P, PACK], BF16, name="pr%d" % n, align_bytes=64)
            pr[i, g] = p
            nc.vector.tensor_tensor(
                out=p[:],
                in0=xt[i, g][:].rearrange("p c t n -> p c n t"),
                in1=hs[:, g : g + n, :].unsqueeze(2).to_broadcast([P, n, P, PACK]),
                op=ALU.mult,
            )

        def quant(i, g, n=1):
            if i >= NT:
                return
            if g == 0:
                hq[i] = small.tile([P, NG, P], U32, name="hq", align_bytes=64)
                hqs[i] = small.tile([P, NG, P], U8, name="hqs", align_bytes=64)
            nc.vector.quantize_mx(
                out=hq[i][:, g : g + n, :].rearrange("p c n -> p (c n)").bitcast(FP8X4),
                scales=hqs[i][:, g : g + n, :].rearrange("p c n -> p (c n)"),
                in_=pr[i, g][:].rearrange("p c n t -> p (c n t)"),
            )

        def mm1(i, g):
            if i >= NT:
                return
            if g == 0:
                kv[i] = ps_kv.tile([P, LAT], F32, name="kv")
                rp[i] = ps_r.tile([P, ROPE], F32, name="rp")
            for dst, c0, c1 in ((kv[i], 0, LAT), (rp[i], LAT, LAT + ROPE)):
                nc.tensor.matmul_mx(
                    out=dst[:],
                    lhsT=hq[i][:, g, :].bitcast(FP8X4),
                    lhsT_scale=hqs[i][:, g, :],
                    rhs=wa[g][:, c0:c1].bitcast(FP8X4),
                    rhs_scale=wa_s[4 * g :, c0:c1],
                    start=(g == 0),
                    stop=(g == NG - 1),
                )

        kt = [outs.tile([P, HEADS, NOPE if i in DIRECT else HEAD], F32, name="kt%d" % i, bufs=1) for i in range(NT)]
        vt = [outs.tile([P, HEADS, VD], F32, name="vt%d" % i, bufs=1) for i in range(NT)]

        def rope(i):
            xr = small.tile([P, ROPE // 2, 2], F32, name="xr")
            nc.scalar.copy(out=xr[:].rearrange("p f e -> p (f e)"), in_=rp[i][:])
            xc = small.tile([P, ROPE // 2, 2], F32, name="xc")
            xs = small.tile([P, ROPE // 2, 2], F32, name="xs")
            r = small.tile([P, ROPE // 2, 2], F32, name="r")
            wide = [P, ROPE // 2, 2]
            nc.gpsimd.tensor_tensor(out=xc[:], in0=xr[:], in1=cos_t[:, i, :].unsqueeze(2).to_broadcast(wide), op=ALU.mult)
            nc.gpsimd.tensor_tensor(out=xs[:], in0=xr[:], in1=sin_t[:, i, :].unsqueeze(2).to_broadcast(wide), op=ALU.mult)
            nc.gpsimd.tensor_tensor(out=r[:, :, 0], in0=xc[:, :, 0], in1=xs[:, :, 1], op=ALU.subtract)
            nc.gpsimd.tensor_tensor(out=r[:, :, 1], in0=xs[:, :, 0], in1=xc[:, :, 1], op=ALU.add)
            if i in DIRECT:
                flat = r[:].rearrange("p f e -> p (f e)").unsqueeze(1).to_broadcast([P, HEADS, ROPE])
                nc.sync.dma_start(out=k_rows[:, i, :, NOPE:], in_=flat)
                return
            flat = r[:].rearrange("p f e -> p (f e)").unsqueeze(1).to_broadcast([P, 4, ROPE])
            for h in range(0, HEADS, 4):
                nc.gpsimd.tensor_scalar(
                    out=kt[i][:, h : h + 4, NOPE:], in0=flat, scalar1=1.0, scalar2=0.0, op0=ALU.mult, op1=ALU.add
                )

        def stats(i):
            st = small.tile([P, 6], F32, name="st")
            nc.vector.bn_stats(out=st[:], in_=kv[i][:])
            return st

        def aggr(i, st):
            mv[i] = small.tile([P, 2], F32, name="mv")
            nc.vector.bn_aggr(out=mv[i][:], in_=st[:])
            rs[i] = small.tile([P, 1], F32, name="rs")
            nc.scalar.activation(out=rs[i][:], in_=mv[i][:, 1:2], func=ACT.Abs_reciprocal_sqrt, bias=EPS)

        def norm1(i):
            y1[i] = small.tile([P, LAT], F32, name="y1")
            nc.vector.scalar_tensor_tensor(
                out=y1[i][:], in0=kv[i][:], scalar=mv[i][:, 0:1], in1=gam, op0=ALU.subtract, op1=ALU.mult
            )

        def norm2(i):
            lat[i] = small.tile([P, LAT], BF16, name="lat")
            nc.vector.scalar_tensor_tensor(
                out=lat[i][:], in0=y1[i][:], scalar=rs[i][:], in1=bet, op0=ALU.mult, op1=ALU.add
            )

        def lat_turn(i):
            lt[i] = ps_x.tile([P, 2, P], F32, name="lt", tag="xt")
            words = lat[i][:].bitcast(F32)
            for j in range(2):
                nc.tensor.transpose(lt[i][:, j, :], words[:, j : LAT // 2 : 2], ident32[:])

        def lat_copy(i):
            lg[i] = small.tile([P, P, 2], F32, name="lg", align_bytes=64)
            nc.scalar.copy(out=lg[i][:], in_=lt[i][:].rearrange("p t n -> p n t"))

        def lat_quant(i):
            lq[i] = small.tile([P, P], U32, name="lq", align_bytes=64)
            lqs[i] = small.tile([P, P], U8, name="lqs", align_bytes=64)
            nc.vector.quantize_mx(out=lq[i][:].bitcast(FP8X4), scales=lqs[i][:], in_=lg[i][:].rearrange("p n t -> p (n t)").bitcast(BF16))

        def mm2(i, out, c0, n):
            nc.tensor.matmul_mx(
                out=out,
                lhsT=lq[i][:].bitcast(FP8X4),
                lhsT_scale=lqs[i][:],
                rhs=wb[:, c0 : c0 + n].bitcast(FP8X4),
                rhs_scale=wb_s[:, c0 : c0 + n],
                start=True,
                stop=True,
            )

        ob = {}
        banks = (("k", 0), ("v", 0), ("k", 1), ("v", 1), ("v", 2), ("v", 3))

        def up(i, b):
            kind, n = banks[b]
            o = ps_o.tile([P, LAT], F32, name="o", tag="o")
            ob[i, b] = o
            mm2(i, o[:], 512 * n + (nn if kind == "v" else 0), 512)

        def out(i, b, eng=None):
            kind, n = banks[b]
            if kind == "v":
                dst = vt[i][:, 4 * n : 4 * n + 4, :]
                src = ob[i, b][:].rearrange("p (h d) -> p h d", d=VD)
            else:
                dst = kt[i][:, 8 * n : 8 * n + 8, 0:NOPE]
                src = ob[i, b][:].rearrange("p (h d) -> p h d", d=NOPE)
            if eng is None:
                nc.scalar.copy(out=dst, in_=src)
            else:
                eng.tensor_copy(out=dst, in_=src)
            if b == 0 and i > 0:
                store(k_rows, kt, i, 0, 8)
            if b == 1 and i == 0:
                store(v_rows, vt, i, 0, 4)
            if b == 2:
                store(k_rows, kt, i, 8 if i > 0 else 0, 16)
            if b == 3:
                store(v_rows, vt, i, 0 if i else 4, 8)
            if b == (5 if i in (0, NT - 1) else 4):
                store(v_rows, vt, i, 8, 16)

        def store(dst, t, i, h0, h1):
            d = t[i].shape[-1]
            nc.sync.dma_start(out=dst[:, i, h0:h1, 0:d], in_=t[i][:, h0:h1, :])

        widen(0, 0, 1, nc.vector)
        widen(0, 1, 1, nc.vector)
        widen(0, 2)
        widen(0, 3)
        turn(0, 0)
        scale(0, 0)
        turn(0, 1)
        warm_up(2)
        scale(0, 1)
        turn(0, 2)
        scale(0, 2)
        quant(0, 0)
        turn(0, 3)
        scale(0, 3)
        for g in range(1, NG):
            quant(0, g)
        for g in range(NG):
            widen(1, g)
        turn(1, 0)
        mm1(0, 0)
        turn(1, 1)
        mm1(0, 1)
        for j in range(2):
            g_ps = ps_o.tile([P, LAT], F32, name="o", tag="o")
            nc.tensor.matmul(out=g_ps[:], lhsT=ones[:], rhs=gb_row[:, j, :], start=True, stop=True)
            nc.scalar.copy(out=gb[:, j, :], in_=g_ps[:])
        widen(2, 0)
        turn(1, 2)
        mm1(0, 2)
        mm1(0, 3)
        rope(0)
        widen(2, 1)
        widen(2, 2)
        scale(1, 0)
        turn(1, 3)
        scale(1, 1)
        turn(2, 0)
        quant(1, 0)
        scale(1, 2)
        turn(2, 1)
        warm_up(2)

        for i in range(NT):
            h, j, k, l = i - 1, i + 1, i + 2, i + 3
            st = stats(i)
            quant(j, 1)
            aggr(i, st)
            quant(j, 2)
            if i == 0:
                widen(2, 3)
                widen(3, 0)
            else:
                out(h, 2)
                out(h, 3)
            norm1(i)
            mm1(j, 0)
            mm1(j, 1)
            if i > 0:
                up(h, 4)
            if i == 1:
                out(h, 4)
            scale(j, 3)
            norm2(i)
            lat_turn(i)
            lat_copy(i)
            scale(k, 0)
            turn(k, 2)
            if i > 0:
                up(h, 5)
            if i == 0:
                widen(3, 1)
                widen(3, 2)
            else:
                out(h, 5)
            if i == 1:
                widen(3, 3)
            quant(j, 3)
            quant(k, 0)
            scale(k, 1)
            lat_quant(i)
            mm1(j, 2)
            mm1(j, 3)
            if j < NT:
                rope(j)
            up(i, 0)
            out(i, 0)
            scale(k, 2)
            if h > 0:
                out(h, 4, nc.vector)
            up(i, 1)
            out(i, 1)
            up(i, 2)
            turn(k, 3)
            turn(l, 0)
            turn(l, 1)
            up(i, 3)
        i = NT - 1
        out(i, 3, nc.vector)
        out(i, 2)
        up(i, 4)
        out(i, 4, nc.vector)
        up(i, 5)
        out(i, 5)
